import numpy as np
import ml_dtypes


def mxq(x, axis, fmt="e4m3"):
    dtype, down = {"e4m3": (ml_dtypes.float8_e4m3fn, 7), "e5m2": (ml_dtypes.float8_e5m2, 14)}[fmt]
    v = np.moveaxis(np.asarray(x, np.float32).astype(ml_dtypes.bfloat16).astype(np.float64), axis, -1)
    blocks = v.reshape(v.shape[:-1] + (-1, 32))
    amax = np.abs(blocks).max(-1, keepdims=True)
    byte = np.maximum(np.where(amax > 0, np.frexp(amax)[1] - 1 + 127, 0) - down, 1)
    scale = np.exp2(byte - 127.0)
    codes = (blocks / scale).astype(np.float32).astype(dtype).astype(np.float64)
    return np.moveaxis((codes * scale).reshape(v.shape), -1, axis)


WIDE = False


def mx_kscale(k):
    if not WIDE:
        return np.ones(k)
    levels = np.array([10, -10, 5, -5, 0])
    a = np.random.permutation(np.resize(levels, k // 512 * 4)).reshape(k // 512, 4)
    idx = np.arange(k)
    return np.exp2(a[idx // 512, idx % 128 // 32])


BF16 = ml_dtypes.bfloat16


def bf(x):
    return np.asarray(x, np.float32).astype(BF16)


def f64(x):
    return np.asarray(x).astype(np.float64)


B, L, C, KS, NL, BH, R = 1, 128, 512, 4, 24, 8, 4
OUT = 2 * BH * NL


def setup_inputs():
    s, t = mx_kscale(C), mx_kscale(C)
    return {"local_features": bf(np.random.standard_normal((B, L, C)) * s),
            "wt": bf(np.random.standard_normal((C, C, KS)) / np.sqrt(C) / s[:, None, None] * t[None, :, None]),
            "bt": bf(np.random.standard_normal(C) * 0.5 * t),
            "w1": bf(np.random.standard_normal((OUT, C)) / np.sqrt(C) / t[None, :]),
            "b1": bf(np.random.standard_normal(OUT) * 0.5)}


def reference(local_features, wt, bt, w1, b1):
    xq = mxq(f64(local_features), 2, "e4m3")
    wq = mxq(f64(wt), 0, "e4m3")
    up = xq @ wq.reshape(C, C * KS)
    up = up.reshape(B, L, C, KS).transpose(0, 2, 1, 3).reshape(B, C, L * KS) + f64(bt)[None, :, None]
    y = (mxq(f64(w1), 1, "e4m3") @ mxq(up, 1, "e4m3")) + f64(b1)[None, :, None]
    y = np.tile(y, (1, 1, R))
    y = y.reshape(B, NL, 2 * BH, L * KS * R)
    return np.ascontiguousarray(y.transpose(2, 0, 1, 3))

@@ -1,0 +1,190 @@
+from contextlib import ExitStack
+
+import concourse.mybir as mybir
+from concourse.masks import make_identity
+
+BF16 = mybir.dt.bfloat16
+F32 = mybir.dt.float32
+U32 = mybir.dt.uint32
+U8 = mybir.dt.uint8
+FP8X4 = mybir.dt.float8_e4m3fn_x4
+IDENTITY = mybir.ActivationFunctionType.Identity
+
+P = 128
+PACK = 4
+L = 128
+C = 512
+TAPS = 4
+T = L * TAPS
+OUT = 384
+REPEAT = 4
+HEADS = 16
+O_TILES = C // P
+Y_TILES = OUT // P
+BIAS_BLOCKS = O_TILES + Y_TILES
+
+WT_VECTOR_COLS = 88
+UP_VECTOR_STEPS = 384
+
+FLOPS = 2 * L * C * C * TAPS + 2 * OUT * C * T
+
+
+def tile_conditionalfeaturesupsample_s_kernel(tc, local_features, wt, bt, w1, b1, out):
+    nc = tc.nc
+    with ExitStack() as ctx:
+        const = ctx.enter_context(tc.tile_pool(name="const", bufs=1))
+        chunks = ctx.enter_context(tc.tile_pool(name="chunks", bufs=O_TILES))
+        results = ctx.enter_context(tc.tile_pool(name="results", bufs=Y_TILES))
+        psum_t = ctx.enter_context(tc.psum_pool(name="psum_t", bufs=Y_TILES))
+        psum_up = ctx.enter_context(tc.psum_pool(name="psum_up", bufs=2))
+        psum_y = ctx.enter_context(tc.psum_pool(name="psum_y", bufs=Y_TILES))
+
+        bias_rows = const.tile([P, BIAS_BLOCKS * P], BF16)
+        nc.vector.memset(bias_rows[:], 0.0)
+        nc.sync.dma_start(out=bias_rows[0:1, 0:C], in_=bt.rearrange("(a c) -> a c", a=1))
+        b1_row = const.tile([1, OUT], BF16)
+        nc.sync.dma_start(out=b1_row[:], in_=b1.rearrange("(a c) -> a c", a=1))
+        x_sb = const.tile([P, C], BF16)
+        nc.sync.dma_start(out=x_sb[:], in_=local_features[0])
+        wt_rows = wt.rearrange("(t p) o k -> p t (o k)", p=P)
+        chunk_cols = P * TAPS
+        wt_raw_tiles = []
+        for h in range(O_TILES):
+            wt_raw = chunks.tile([P, PACK, chunk_cols], BF16)
+            nc.sync.dma_start(out=wt_raw[:], in_=wt_rows[:, :, h * chunk_cols : (h + 1) * chunk_cols])
+            wt_raw_tiles.append(wt_raw)
+        w1_sb = const.tile([P, Y_TILES, C], BF16)
+        nc.sync.dma_start(out=w1_sb[:], in_=w1.rearrange("(a r) o -> r a o", r=P))
+
+        ident = const.tile([P, P], BF16)
+        make_identity(nc, ident[:])
+
+        x_ps = psum_t.tile([P, PACK, L], BF16, tag="transposed")
+        for t in range(PACK):
+            nc.tensor.transpose(x_ps[:, t, :], x_sb[:, t * P : (t + 1) * P], ident[:])
+        x_grouped = const.tile([P, L, PACK], BF16, align_bytes=64)
+        nc.vector.tensor_copy(out=x_grouped[:], in_=x_ps[:].rearrange("p t l -> p l t"))
+        x_codes = const.tile([P, L], U32, align_bytes=64)
+        x_scales = const.tile([P, L], U8, align_bytes=64)
+        nc.vector.quantize_mx(
+            out=x_codes[:].bitcast(FP8X4),
+            scales=x_scales[:],
+            in_=x_grouped[:].rearrange("p l t -> p (l t)"),
+        )
+
+        nc.vector.tensor_copy(
+            out=bias_rows[0:1, C : C + OUT].rearrange("a (j n) -> a j n", j=HEADS),
+            in_=b1_row[:].rearrange("a (n j) -> a j n", j=HEADS),
+        )
+        bias_ps = psum_t.tile([P, BIAS_BLOCKS, P], BF16, tag="transposed")
+        for blk in range(BIAS_BLOCKS):
+            nc.tensor.transpose(bias_ps[:, blk, :], bias_rows[:, blk * P : (blk + 1) * P], ident[:])
+        bias_cols = const.tile([P, BIAS_BLOCKS], F32)
+        nc.vector.tensor_copy(out=bias_cols[:], in_=bias_ps[:, :, 0])
+
+        w1_codes = const.tile([P, OUT], U32, align_bytes=64)
+        w1_scales = const.tile([P, OUT], U8, align_bytes=64)
+
+        def prepare_w1():
+            w1_grouped = const.tile([P, OUT, PACK], BF16, align_bytes=64)
+            w1_by_head = w1_grouped[:].rearrange("p (j n) t -> p j n t", j=HEADS)
+            layers_per_tile = P // HEADS
+            for a in range(Y_TILES):
+                w1_ps = psum_t.tile([P, PACK, P], BF16, tag="transposed")
+                for t in range(PACK):
+                    nc.tensor.transpose(w1_ps[:, t, :], w1_sb[:, a, t * P : (t + 1) * P], ident[:])
+                nc.scalar.copy(
+                    out=w1_by_head[:, :, a * layers_per_tile : (a + 1) * layers_per_tile, :],
+                    in_=w1_ps[:].rearrange("p t (n j) -> p j n t", j=HEADS),
+                )
+            for a in range(Y_TILES):
+                rows = slice(a * P, (a + 1) * P)
+                nc.vector.quantize_mx(
+                    out=w1_codes[:, rows].bitcast(FP8X4),
+                    scales=w1_scales[:, rows],
+                    in_=w1_grouped[:, rows, :].rearrange("p q t -> p (q t)"),
+                )
+
+        def regroup_wt(h):
+            wt_grouped = chunks.tile([P, TAPS, P, PACK], BF16, align_bytes=64)
+            src = wt_raw_tiles[h][:].rearrange("p t (m k) -> p m t k", k=TAPS)
+            dst = wt_grouped[:].rearrange("p k m t -> p m t k")
+            nc.vector.tensor_copy(out=dst[:, 0:WT_VECTOR_COLS], in_=src[:, 0:WT_VECTOR_COLS])
+            nc.scalar.copy(out=dst[:, WT_VECTOR_COLS:P], in_=src[:, WT_VECTOR_COLS:P])
+            return wt_grouped
+
+        up_planes = const.tile([P, O_TILES, T], BF16)
+
+        def convolve(h, wt_grouped, before_multiply):
+            wt_codes = chunks.tile([P, TAPS, P], U32, align_bytes=64)
+            wt_scales = chunks.tile([P, TAPS, P], U8, align_bytes=64)
+            nc.vector.quantize_mx(
+                out=wt_codes[:].rearrange("p k m -> p (k m)").bitcast(FP8X4),
+                scales=wt_scales[:].rearrange("p k m -> p (k m)"),
+                in_=wt_grouped[:].rearrange("p k m t -> p (k m t)"),
+            )
+            before_multiply()
+            up_ps = psum_up.tile([P, TAPS, L], F32)
+            for k in range(TAPS):
+                nc.tensor.matmul_mx(
+                    out=up_ps[:, k, :],
+                    lhsT=wt_codes[:, k, :].bitcast(FP8X4),
+                    lhsT_scale=wt_scales[:, k, :],
+                    rhs=x_codes[:].bitcast(FP8X4),
+                    rhs_scale=x_scales[:],
+                    start=True,
+                    stop=True,
+                )
+            nc.scalar.activation(
+                out=up_planes[:, h, :].rearrange("p (l k) -> p l k", k=TAPS),
+                in_=up_ps[:].rearrange("p k l -> p l k"),
+                func=IDENTITY,
+                bias=bias_cols[:, h : h + 1],
+            )
+
+        def nothing():
+            return None
+
+        grouped_next = regroup_wt(0)
+        for h in range(O_TILES):
+            grouped_now = grouped_next
+            last = h == O_TILES - 1
+            if not last:
+                grouped_next = regroup_wt(h + 1)
+            convolve(h, grouped_now, prepare_w1 if last else nothing)
+
+        up_grouped = const.tile([P, T, PACK], BF16, align_bytes=64)
+        src = up_planes[:].rearrange("p h (c i) -> p c h i", i=4)
+        dst = up_grouped[:].rearrange("p (c i) h -> p c h i", i=4)
+        split = UP_VECTOR_STEPS // 4
+        nc.vector.tensor_copy(out=dst[:, 0:split], in_=src[:, 0:split])
+        nc.scalar.copy(out=dst[:, split : T // 4], in_=src[:, split : T // 4])
+        up_codes = const.tile([P, T], U32, align_bytes=64)
+        up_scales = const.tile([P, T], U8, align_bytes=64)
+        nc.vector.quantize_mx(
+            out=up_codes[:].bitcast(FP8X4),
+            scales=up_scales[:],
+            in_=up_grouped[:].rearrange("p s h -> p (s h)"),
+        )
+
+        out_rows = out.rearrange("j b n s -> (j b n) s")
+        for a in range(Y_TILES):
+            rows = slice(a * P, (a + 1) * P)
+            y_ps = psum_y.tile([P, T], F32)
+            nc.tensor.matmul_mx(
+                out=y_ps[:],
+                lhsT=w1_codes[:, rows].bitcast(FP8X4),
+                lhsT_scale=w1_scales[:, rows],
+                rhs=up_codes[:].bitcast(FP8X4),
+                rhs_scale=up_scales[:],
+                start=True,
+                stop=True,
+            )
+            y_sb = results.tile([P, T], F32)
+            b1_col = bias_cols[:, O_TILES + a : O_TILES + a + 1]
+            if a % 2 == 0:
+                nc.vector.tensor_scalar_add(out=y_sb[:], in0=y_ps[:], scalar1=b1_col)
+            else:
+                nc.scalar.activation(out=y_sb[:], in_=y_ps[:], func=IDENTITY, bias=b1_col)
+            for r in range(REPEAT):
+                nc.sync.dma_start(out=out_rows[rows, r * T : (r + 1) * T], in_=y_sb[:])

@@ -22,9 +22,14 @@ HEADS = 16
 O_TILES = C // P
 Y_TILES = OUT // P
 BIAS_BLOCKS = O_TILES + Y_TILES
+HALVES = 2
+HALF_TAPS = TAPS // HALVES
+HALF_T = T // HALVES
+UNITS = O_TILES * HALVES
 
 WT_VECTOR_COLS = 88
-UP_VECTOR_STEPS = 384
+UP_VECTOR_STEPS = 192
+CHUNKS_BEFORE_W1 = 2
 
 FLOPS = 2 * L * C * C * TAPS + 2 * OUT * C * T
 
@@ -32,29 +37,32 @@ FLOPS = 2 * L * C * C * TAPS + 2 * OUT * C * T
 def tile_conditionalfeaturesupsample_s_kernel(tc, local_features, wt, bt, w1, b1, out):
     nc = tc.nc
     with ExitStack() as ctx:
+        ctx.enter_context(tc.manual_schedule())
         const = ctx.enter_context(tc.tile_pool(name="const", bufs=1))
         chunks = ctx.enter_context(tc.tile_pool(name="chunks", bufs=O_TILES))
+        units = ctx.enter_context(tc.tile_pool(name="units", bufs=UNITS))
         results = ctx.enter_context(tc.tile_pool(name="results", bufs=Y_TILES))
         psum_t = ctx.enter_context(tc.psum_pool(name="psum_t", bufs=Y_TILES))
         psum_up = ctx.enter_context(tc.psum_pool(name="psum_up", bufs=2))
         psum_y = ctx.enter_context(tc.psum_pool(name="psum_y", bufs=Y_TILES))
 
+        x_sb = const.tile([P, C], BF16)
+        nc.sync.dma_start(out=x_sb[:], in_=local_features[0])
         bias_rows = const.tile([P, BIAS_BLOCKS * P], BF16)
         nc.vector.memset(bias_rows[:], 0.0)
         nc.sync.dma_start(out=bias_rows[0:1, 0:C], in_=bt.rearrange("(a c) -> a c", a=1))
         b1_row = const.tile([1, OUT], BF16)
         nc.sync.dma_start(out=b1_row[:], in_=b1.rearrange("(a c) -> a c", a=1))
-        x_sb = const.tile([P, C], BF16)
-        nc.sync.dma_start(out=x_sb[:], in_=local_features[0])
         wt_rows = wt.rearrange("(t p) o k -> p t (o k)", p=P)
         chunk_cols = P * TAPS
+        w1_sb = const.tile([P, Y_TILES, C], BF16)
         wt_raw_tiles = []
         for h in range(O_TILES):
+            if h == CHUNKS_BEFORE_W1:
+                nc.sync.dma_start(out=w1_sb[:], in_=w1.rearrange("(a r) o -> r a o", r=P))
             wt_raw = chunks.tile([P, PACK, chunk_cols], BF16)
             nc.sync.dma_start(out=wt_raw[:], in_=wt_rows[:, :, h * chunk_cols : (h + 1) * chunk_cols])
             wt_raw_tiles.append(wt_raw)
-        w1_sb = const.tile([P, Y_TILES, C], BF16)
-        nc.sync.dma_start(out=w1_sb[:], in_=w1.rearrange("(a r) o -> r a o", r=P))
 
         ident = const.tile([P, P], BF16)
         make_identity(nc, ident[:])
@@ -80,23 +88,30 @@ def tile_conditionalfeaturesupsample_s_kernel(tc, local_features, wt, bt, w1, b1
         for blk in range(BIAS_BLOCKS):
             nc.tensor.transpose(bias_ps[:, blk, :], bias_rows[:, blk * P : (blk + 1) * P], ident[:])
         bias_cols = const.tile([P, BIAS_BLOCKS], F32)
-        nc.vector.tensor_copy(out=bias_cols[:], in_=bias_ps[:, :, 0])
 
         w1_codes = const.tile([P, OUT], U32, align_bytes=64)
         w1_scales = const.tile([P, OUT], U8, align_bytes=64)
 
-        def prepare_w1():
-            w1_grouped = const.tile([P, OUT, PACK], BF16, align_bytes=64)
-            w1_by_head = w1_grouped[:].rearrange("p (j n) t -> p j n t", j=HEADS)
-            layers_per_tile = P // HEADS
+        w1_grouped = const.tile([P, OUT, PACK], BF16, align_bytes=64)
+        w1_ps_tiles = []
+
+        def transpose_w1():
             for a in range(Y_TILES):
                 w1_ps = psum_t.tile([P, PACK, P], BF16, tag="transposed")
                 for t in range(PACK):
                     nc.tensor.transpose(w1_ps[:, t, :], w1_sb[:, a, t * P : (t + 1) * P], ident[:])
+                w1_ps_tiles.append(w1_ps)
+
+        def regroup_w1():
+            w1_by_head = w1_grouped[:].rearrange("p (j n) t -> p j n t", j=HEADS)
+            layers_per_tile = P // HEADS
+            for a in range(Y_TILES):
                 nc.scalar.copy(
                     out=w1_by_head[:, :, a * layers_per_tile : (a + 1) * layers_per_tile, :],
-                    in_=w1_ps[:].rearrange("p t (n j) -> p j n t", j=HEADS),
+                    in_=w1_ps_tiles[a][:].rearrange("p t (n j) -> p j n t", j=HEADS),
                 )
+
+        def quantise_w1():
             for a in range(Y_TILES):
                 rows = slice(a * P, (a + 1) * P)
                 nc.vector.quantize_mx(
@@ -105,27 +120,26 @@ def tile_conditionalfeaturesupsample_s_kernel(tc, local_features, wt, bt, w1, b1
                     in_=w1_grouped[:, rows, :].rearrange("p q t -> p (q t)"),
                 )
 
-        def regroup_wt(h):
-            wt_grouped = chunks.tile([P, TAPS, P, PACK], BF16, align_bytes=64)
-            src = wt_raw_tiles[h][:].rearrange("p t (m k) -> p m t k", k=TAPS)
+        def regroup_wt(u):
+            h, half = divmod(u, HALVES)
+            taps = slice(half * HALF_TAPS, (half + 1) * HALF_TAPS)
+            wt_grouped = units.tile([P, HALF_TAPS, P, PACK], BF16, align_bytes=64)
+            src = wt_raw_tiles[h][:].rearrange("p t (m k) -> p m t k", k=TAPS)[:, :, :, taps]
             dst = wt_grouped[:].rearrange("p k m t -> p m t k")
             nc.vector.tensor_copy(out=dst[:, 0:WT_VECTOR_COLS], in_=src[:, 0:WT_VECTOR_COLS])
             nc.scalar.copy(out=dst[:, WT_VECTOR_COLS:P], in_=src[:, WT_VECTOR_COLS:P])
             return wt_grouped
 
-        up_planes = const.tile([P, O_TILES, T], BF16)
-
-        def convolve(h, wt_grouped, before_multiply):
-            wt_codes = chunks.tile([P, TAPS, P], U32, align_bytes=64)
-            wt_scales = chunks.tile([P, TAPS, P], U8, align_bytes=64)
+        def quantise_and_multiply(wt_grouped):
+            wt_codes = units.tile([P, HALF_TAPS, P], U32, align_bytes=64)
+            wt_scales = units.tile([P, HALF_TAPS, P], U8, align_bytes=64)
             nc.vector.quantize_mx(
                 out=wt_codes[:].rearrange("p k m -> p (k m)").bitcast(FP8X4),
                 scales=wt_scales[:].rearrange("p k m -> p (k m)"),
                 in_=wt_grouped[:].rearrange("p k m t -> p (k m t)"),
             )
-            before_multiply()
-            up_ps = psum_up.tile([P, TAPS, L], F32)
-            for k in range(TAPS):
+            up_ps = psum_up.tile([P, HALF_TAPS, L], F32)
+            for k in range(HALF_TAPS):
                 nc.tensor.matmul_mx(
                     out=up_ps[:, k, :],
                     lhsT=wt_codes[:, k, :].bitcast(FP8X4),
@@ -135,56 +149,74 @@ def tile_conditionalfeaturesupsample_s_kernel(tc, local_features, wt, bt, w1, b1
                     start=True,
                     stop=True,
                 )
+            return up_ps
+
+        up_planes = const.tile([P, HALVES, O_TILES, HALF_T], BF16)
+
+        def add_bt(u, up_ps):
+            h, half = divmod(u, HALVES)
             nc.scalar.activation(
-                out=up_planes[:, h, :].rearrange("p (l k) -> p l k", k=TAPS),
-                in_=up_ps[:].rearrange("p k l -> p l k"),
+                out=up_planes[:, half, h, :],
+                in_=up_ps[:].rearrange("p k l -> p (k l)"),
                 func=IDENTITY,
                 bias=bias_cols[:, h : h + 1],
             )
 
-        def nothing():
-            return None
+        grouped_tiles = [regroup_wt(0)]
+        nc.scalar.copy(out=bias_cols[:], in_=bias_ps[:, :, 0])
+        up_ps_tiles = []
+        for u in range(UNITS):
+            if u + 1 < UNITS:
+                grouped_tiles.append(regroup_wt(u + 1))
+            up_ps_tiles.append(quantise_and_multiply(grouped_tiles[u]))
+            if u >= 1:
+                add_bt(u - 1, up_ps_tiles[u - 1])
+            if u + 1 == CHUNKS_BEFORE_W1 * HALVES:
+                transpose_w1()
+            if u == CHUNKS_BEFORE_W1 * HALVES:
+                regroup_w1()
+        quantise_w1()
 
-        grouped_next = regroup_wt(0)
-        for h in range(O_TILES):
-            grouped_now = grouped_next
-            last = h == O_TILES - 1
-            if not last:
-                grouped_next = regroup_wt(h + 1)
-            convolve(h, grouped_now, prepare_w1 if last else nothing)
-
-        up_grouped = const.tile([P, T, PACK], BF16, align_bytes=64)
-        src = up_planes[:].rearrange("p h (c i) -> p c h i", i=4)
-        dst = up_grouped[:].rearrange("p (c i) h -> p c h i", i=4)
-        split = UP_VECTOR_STEPS // 4
-        nc.vector.tensor_copy(out=dst[:, 0:split], in_=src[:, 0:split])
-        nc.scalar.copy(out=dst[:, split : T // 4], in_=src[:, split : T // 4])
+        up_grouped = const.tile([P, HALVES, HALF_T, PACK], BF16, align_bytes=64)
         up_codes = const.tile([P, T], U32, align_bytes=64)
         up_scales = const.tile([P, T], U8, align_bytes=64)
-        nc.vector.quantize_mx(
-            out=up_codes[:].bitcast(FP8X4),
-            scales=up_scales[:],
-            in_=up_grouped[:].rearrange("p s h -> p (s h)"),
-        )
+        src = up_planes[:].rearrange("p f h (c i) -> p f c h i", i=4)
+        dst = up_grouped[:].rearrange("p f (c i) h -> p f c h i", i=4)
+        split = UP_VECTOR_STEPS // 4
+        nc.vector.tensor_copy(out=dst[:, 0], in_=src[:, 0])
+        add_bt(UNITS - 1, up_ps_tiles[UNITS - 1])
+        nc.vector.tensor_copy(out=dst[:, 1, 0:split], in_=src[:, 1, 0:split])
+        nc.scalar.copy(out=dst[:, 1, split : HALF_T // 4], in_=src[:, 1, split : HALF_T // 4])
+        for half in range(HALVES):
+            steps = slice(half * HALF_T, (half + 1) * HALF_T)
+            nc.vector.quantize_mx(
+                out=up_codes[:, steps].bitcast(FP8X4),
+                scales=up_scales[:, steps],
+                in_=up_grouped[:, half].rearrange("p s h -> p (s h)"),
+            )
 
         out_rows = out.rearrange("j b n s -> (j b n) s")
         for a in range(Y_TILES):
             rows = slice(a * P, (a + 1) * P)
             y_ps = psum_y.tile([P, T], F32)
-            nc.tensor.matmul_mx(
-                out=y_ps[:],
-                lhsT=w1_codes[:, rows].bitcast(FP8X4),
-                lhsT_scale=w1_scales[:, rows],
-                rhs=up_codes[:].bitcast(FP8X4),
-                rhs_scale=up_scales[:],
-                start=True,
-                stop=True,
-            )
+            for half in range(HALVES):
+                steps = slice(half * HALF_T, (half + 1) * HALF_T)
+                nc.tensor.matmul_mx(
+                    out=y_ps[:, steps],
+                    lhsT=w1_codes[:, rows].bitcast(FP8X4),
+                    lhsT_scale=w1_scales[:, rows],
+                    rhs=up_codes[:, steps].bitcast(FP8X4),
+                    rhs_scale=up_scales[:, steps],
+                    start=True,
+                    stop=True,
+                )
             y_sb = results.tile([P, T], F32)
+            y_in_time = y_sb[:].rearrange("p (l k) -> p l k", k=TAPS)
+            y_by_tap = y_ps[:].rearrange("p (k l) -> p l k", k=TAPS)
             b1_col = bias_cols[:, O_TILES + a : O_TILES + a + 1]
             if a % 2 == 0:
-                nc.vector.tensor_scalar_add(out=y_sb[:], in0=y_ps[:], scalar1=b1_col)
+                nc.vector.tensor_scalar_add(out=y_in_time, in0=y_by_tap, scalar1=b1_col)
             else:
-                nc.scalar.activation(out=y_sb[:], in_=y_ps[:], func=IDENTITY, bias=b1_col)
+                nc.scalar.activation(out=y_in_time, in_=y_by_tap, func=IDENTITY, bias=b1_col)
             for r in range(REPEAT):
                 nc.sync.dma_start(out=out_rows[rows, r * T : (r + 1) * T], in_=y_sb[:])

@@ -25,9 +25,11 @@ BIAS_BLOCKS = O_TILES + Y_TILES
 HALVES = 2
 HALF_TAPS = TAPS // HALVES
 HALF_T = T // HALVES
-UNITS = O_TILES * HALVES
+PIECES = [(h, 0, TAPS) for h in range(O_TILES - 1)] + [
+    (O_TILES - 1, half * HALF_TAPS, HALF_TAPS) for half in range(HALVES)
+]
 
-WT_VECTOR_COLS = 88
+WT_VECTOR_COLS = 72
 UP_VECTOR_STEPS = 192
 CHUNKS_BEFORE_W1 = 2
 
@@ -40,7 +42,7 @@ def tile_conditionalfeaturesupsample_s_kernel(tc, local_features, wt, bt, w1, b1
         ctx.enter_context(tc.manual_schedule())
         const = ctx.enter_context(tc.tile_pool(name="const", bufs=1))
         chunks = ctx.enter_context(tc.tile_pool(name="chunks", bufs=O_TILES))
-        units = ctx.enter_context(tc.tile_pool(name="units", bufs=UNITS))
+        pieces = ctx.enter_context(tc.tile_pool(name="pieces", bufs=len(PIECES)))
         results = ctx.enter_context(tc.tile_pool(name="results", bufs=Y_TILES))
         psum_t = ctx.enter_context(tc.psum_pool(name="psum_t", bufs=Y_TILES))
         psum_up = ctx.enter_context(tc.psum_pool(name="psum_up", bufs=2))
@@ -88,6 +90,7 @@ def tile_conditionalfeaturesupsample_s_kernel(tc, local_features, wt, bt, w1, b1
         for blk in range(BIAS_BLOCKS):
             nc.tensor.transpose(bias_ps[:, blk, :], bias_rows[:, blk * P : (blk + 1) * P], ident[:])
         bias_cols = const.tile([P, BIAS_BLOCKS], F32)
+        nc.scalar.copy(out=bias_cols[:], in_=bias_ps[:, :, 0])
 
         w1_codes = const.tile([P, OUT], U32, align_bytes=64)
         w1_scales = const.tile([P, OUT], U8, align_bytes=64)
@@ -120,26 +123,27 @@ def tile_conditionalfeaturesupsample_s_kernel(tc, local_features, wt, bt, w1, b1
                     in_=w1_grouped[:, rows, :].rearrange("p q t -> p (q t)"),
                 )
 
-        def regroup_wt(u):
-            h, half = divmod(u, HALVES)
-            taps = slice(half * HALF_TAPS, (half + 1) * HALF_TAPS)
-            wt_grouped = units.tile([P, HALF_TAPS, P, PACK], BF16, align_bytes=64)
+        def regroup_wt(piece):
+            h, first_tap, n_taps = piece
+            taps = slice(first_tap, first_tap + n_taps)
+            wt_grouped = pieces.tile([P, n_taps, P, PACK], BF16, align_bytes=64)
             src = wt_raw_tiles[h][:].rearrange("p t (m k) -> p m t k", k=TAPS)[:, :, :, taps]
             dst = wt_grouped[:].rearrange("p k m t -> p m t k")
             nc.vector.tensor_copy(out=dst[:, 0:WT_VECTOR_COLS], in_=src[:, 0:WT_VECTOR_COLS])
             nc.scalar.copy(out=dst[:, WT_VECTOR_COLS:P], in_=src[:, WT_VECTOR_COLS:P])
             return wt_grouped
 
-        def quantise_and_multiply(wt_grouped):
-            wt_codes = units.tile([P, HALF_TAPS, P], U32, align_bytes=64)
-            wt_scales = units.tile([P, HALF_TAPS, P], U8, align_bytes=64)
+        def quantise_and_multiply(piece, wt_grouped):
+            n_taps = piece[2]
+            wt_codes = pieces.tile([P, n_taps, P], U32, align_bytes=64)
+            wt_scales = pieces.tile([P, n_taps, P], U8, align_bytes=64)
             nc.vector.quantize_mx(
                 out=wt_codes[:].rearrange("p k m -> p (k m)").bitcast(FP8X4),
                 scales=wt_scales[:].rearrange("p k m -> p (k m)"),
                 in_=wt_grouped[:].rearrange("p k m t -> p (k m t)"),
             )
-            up_ps = psum_up.tile([P, HALF_TAPS, L], F32)
-            for k in range(HALF_TAPS):
+            up_ps = psum_up.tile([P, n_taps, L], F32)
+            for k in range(n_taps):
                 nc.tensor.matmul_mx(
                     out=up_ps[:, k, :],
                     lhsT=wt_codes[:, k, :].bitcast(FP8X4),
@@ -151,40 +155,39 @@ def tile_conditionalfeaturesupsample_s_kernel(tc, local_features, wt, bt, w1, b1
                 )
             return up_ps
 
-        up_planes = const.tile([P, HALVES, O_TILES, HALF_T], BF16)
+        up_planes = const.tile([P, O_TILES, T], BF16)
 
-        def add_bt(u, up_ps):
-            h, half = divmod(u, HALVES)
+        def add_bt(piece, up_ps):
+            h, first_tap, n_taps = piece
             nc.scalar.activation(
-                out=up_planes[:, half, h, :],
+                out=up_planes[:, h, first_tap * L : (first_tap + n_taps) * L],
                 in_=up_ps[:].rearrange("p k l -> p (k l)"),
                 func=IDENTITY,
                 bias=bias_cols[:, h : h + 1],
             )
 
-        grouped_tiles = [regroup_wt(0)]
-        nc.scalar.copy(out=bias_cols[:], in_=bias_ps[:, :, 0])
+        grouped_tiles = [regroup_wt(PIECES[0])]
         up_ps_tiles = []
-        for u in range(UNITS):
-            if u + 1 < UNITS:
-                grouped_tiles.append(regroup_wt(u + 1))
-            up_ps_tiles.append(quantise_and_multiply(grouped_tiles[u]))
-            if u >= 1:
-                add_bt(u - 1, up_ps_tiles[u - 1])
-            if u + 1 == CHUNKS_BEFORE_W1 * HALVES:
+        for i in range(len(PIECES)):
+            if i + 1 < len(PIECES):
+                grouped_tiles.append(regroup_wt(PIECES[i + 1]))
+            up_ps_tiles.append(quantise_and_multiply(PIECES[i], grouped_tiles[i]))
+            if i >= 1:
+                add_bt(PIECES[i - 1], up_ps_tiles[i - 1])
+            if i + 1 == CHUNKS_BEFORE_W1:
                 transpose_w1()
-            if u == CHUNKS_BEFORE_W1 * HALVES:
+            if i == CHUNKS_BEFORE_W1:
                 regroup_w1()
         quantise_w1()
 
         up_grouped = const.tile([P, HALVES, HALF_T, PACK], BF16, align_bytes=64)
         up_codes = const.tile([P, T], U32, align_bytes=64)
         up_scales = const.tile([P, T], U8, align_bytes=64)
-        src = up_planes[:].rearrange("p f h (c i) -> p f c h i", i=4)
+        src = up_planes[:].rearrange("p h (f c i) -> p f c h i", f=HALVES, i=4)
         dst = up_grouped[:].rearrange("p f (c i) h -> p f c h i", i=4)
         split = UP_VECTOR_STEPS // 4
         nc.vector.tensor_copy(out=dst[:, 0], in_=src[:, 0])
-        add_bt(UNITS - 1, up_ps_tiles[UNITS - 1])
+        add_bt(PIECES[-1], up_ps_tiles[-1])
         nc.vector.tensor_copy(out=dst[:, 1, 0:split], in_=src[:, 1, 0:split])
         nc.scalar.copy(out=dst[:, 1, split : HALF_T // 4], in_=src[:, 1, split : HALF_T // 4])
         for half in range(HALVES):

from contextlib import ExitStack

import concourse.mybir as mybir
from concourse.masks import make_identity

BF16 = mybir.dt.bfloat16
F32 = mybir.dt.float32
U32 = mybir.dt.uint32
U8 = mybir.dt.uint8
FP8X4 = mybir.dt.float8_e4m3fn_x4
IDENTITY = mybir.ActivationFunctionType.Identity

P = 128
PACK = 4
L = 128
C = 512
TAPS = 4
T = L * TAPS
OUT = 384
REPEAT = 4
HEADS = 16
O_TILES = C // P
Y_TILES = OUT // P
BIAS_BLOCKS = O_TILES + Y_TILES
HALVES = 2
HALF_TAPS = TAPS // HALVES
HALF_T = T // HALVES
PIECES = [(h, 0, TAPS) for h in range(O_TILES - 1)] + [
    (O_TILES - 1, half * HALF_TAPS, HALF_TAPS) for half in range(HALVES)
]

WT_VECTOR_COLS = 72
UP_VECTOR_STEPS = 192
CHUNKS_BEFORE_W1 = 2

FLOPS = 2 * L * C * C * TAPS + 2 * OUT * C * T


def tile_conditionalfeaturesupsample_s_kernel(tc, local_features, wt, bt, w1, b1, out):
    nc = tc.nc
    with ExitStack() as ctx:
        ctx.enter_context(tc.manual_schedule())
        const = ctx.enter_context(tc.tile_pool(name="const", bufs=1))
        chunks = ctx.enter_context(tc.tile_pool(name="chunks", bufs=O_TILES))
        pieces = ctx.enter_context(tc.tile_pool(name="pieces", bufs=len(PIECES)))
        results = ctx.enter_context(tc.tile_pool(name="results", bufs=Y_TILES))
        psum_t = ctx.enter_context(tc.psum_pool(name="psum_t", bufs=Y_TILES))
        psum_up = ctx.enter_context(tc.psum_pool(name="psum_up", bufs=2))
        psum_y = ctx.enter_context(tc.psum_pool(name="psum_y", bufs=Y_TILES))

        x_sb = const.tile([P, C], BF16)
        nc.sync.dma_start(out=x_sb[:], in_=local_features[0])
        bias_rows = const.tile([P, BIAS_BLOCKS * P], BF16)
        nc.vector.memset(bias_rows[:], 0.0)
        nc.sync.dma_start(out=bias_rows[0:1, 0:C], in_=bt.rearrange("(a c) -> a c", a=1))
        b1_row = const.tile([1, OUT], BF16)
        nc.sync.dma_start(out=b1_row[:], in_=b1.rearrange("(a c) -> a c", a=1))
        wt_rows = wt.rearrange("(t p) o k -> p t (o k)", p=P)
        chunk_cols = P * TAPS
        w1_sb = const.tile([P, Y_TILES, C], BF16)
        wt_raw_tiles = []
        for h in range(O_TILES):
            if h == CHUNKS_BEFORE_W1:
                nc.sync.dma_start(out=w1_sb[:], in_=w1.rearrange("(a r) o -> r a o", r=P))
            wt_raw = chunks.tile([P, PACK, chunk_cols], BF16)
            nc.sync.dma_start(out=wt_raw[:], in_=wt_rows[:, :, h * chunk_cols : (h + 1) * chunk_cols])
            wt_raw_tiles.append(wt_raw)

        ident = const.tile([P, P], BF16)
        make_identity(nc, ident[:])

        x_ps = psum_t.tile([P, PACK, L], BF16, tag="transposed")
        for t in range(PACK):
            nc.tensor.transpose(x_ps[:, t, :], x_sb[:, t * P : (t + 1) * P], ident[:])
        x_grouped = const.tile([P, L, PACK], BF16, align_bytes=64)
        nc.vector.tensor_copy(out=x_grouped[:], in_=x_ps[:].rearrange("p t l -> p l t"))
        x_codes = const.tile([P, L], U32, align_bytes=64)
        x_scales = const.tile([P, L], U8, align_bytes=64)
        nc.vector.quantize_mx(
            out=x_codes[:].bitcast(FP8X4),
            scales=x_scales[:],
            in_=x_grouped[:].rearrange("p l t -> p (l t)"),
        )

        nc.vector.tensor_copy(
            out=bias_rows[0:1, C : C + OUT].rearrange("a (j n) -> a j n", j=HEADS),
            in_=b1_row[:].rearrange("a (n j) -> a j n", j=HEADS),
        )
        bias_ps = psum_t.tile([P, BIAS_BLOCKS, P], BF16, tag="transposed")
        for blk in range(BIAS_BLOCKS):
            nc.tensor.transpose(bias_ps[:, blk, :], bias_rows[:, blk * P : (blk + 1) * P], ident[:])
        bias_cols = const.tile([P, BIAS_BLOCKS], F32)
        nc.scalar.copy(out=bias_cols[:], in_=bias_ps[:, :, 0])

        w1_codes = const.tile([P, OUT], U32, align_bytes=64)
        w1_scales = const.tile([P, OUT], U8, align_bytes=64)

        w1_grouped = const.tile([P, OUT, PACK], BF16, align_bytes=64)
        w1_ps_tiles = []

        def transpose_w1():
            for a in range(Y_TILES):
                w1_ps = psum_t.tile([P, PACK, P], BF16, tag="transposed")
                for t in range(PACK):
                    nc.tensor.transpose(w1_ps[:, t, :], w1_sb[:, a, t * P : (t + 1) * P], ident[:])
                w1_ps_tiles.append(w1_ps)

        def regroup_w1():
            w1_by_head = w1_grouped[:].rearrange("p (j n) t -> p j n t", j=HEADS)
            layers_per_tile = P // HEADS
            for a in range(Y_TILES):
                nc.scalar.copy(
                    out=w1_by_head[:, :, a * layers_per_tile : (a + 1) * layers_per_tile, :],
                    in_=w1_ps_tiles[a][:].rearrange("p t (n j) -> p j n t", j=HEADS),
                )

        def quantise_w1():
            for a in range(Y_TILES):
                rows = slice(a * P, (a + 1) * P)
                nc.vector.quantize_mx(
                    out=w1_codes[:, rows].bitcast(FP8X4),
                    scales=w1_scales[:, rows],
                    in_=w1_grouped[:, rows, :].rearrange("p q t -> p (q t)"),
                )

        def regroup_wt(piece):
            h, first_tap, n_taps = piece
            taps = slice(first_tap, first_tap + n_taps)
            wt_grouped = pieces.tile([P, n_taps, P, PACK], BF16, align_bytes=64)
            src = wt_raw_tiles[h][:].rearrange("p t (m k) -> p m t k", k=TAPS)[:, :, :, taps]
            dst = wt_grouped[:].rearrange("p k m t -> p m t k")
            nc.vector.tensor_copy(out=dst[:, 0:WT_VECTOR_COLS], in_=src[:, 0:WT_VECTOR_COLS])
            nc.scalar.copy(out=dst[:, WT_VECTOR_COLS:P], in_=src[:, WT_VECTOR_COLS:P])
            return wt_grouped

        def quantise_and_multiply(piece, wt_grouped):
            n_taps = piece[2]
            wt_codes = pieces.tile([P, n_taps, P], U32, align_bytes=64)
            wt_scales = pieces.tile([P, n_taps, P], U8, align_bytes=64)
            nc.vector.quantize_mx(
                out=wt_codes[:].rearrange("p k m -> p (k m)").bitcast(FP8X4),
                scales=wt_scales[:].rearrange("p k m -> p (k m)"),
                in_=wt_grouped[:].rearrange("p k m t -> p (k m t)"),
            )
            up_ps = psum_up.tile([P, n_taps, L], F32)
            for k in range(n_taps):
                nc.tensor.matmul_mx(
                    out=up_ps[:, k, :],
                    lhsT=wt_codes[:, k, :].bitcast(FP8X4),
                    lhsT_scale=wt_scales[:, k, :],
                    rhs=x_codes[:].bitcast(FP8X4),
                    rhs_scale=x_scales[:],
                    start=True,
                    stop=True,
                )
            return up_ps

        up_planes = const.tile([P, O_TILES, T], BF16)

        def add_bt(piece, up_ps):
            h, first_tap, n_taps = piece
            nc.scalar.activation(
                out=up_planes[:, h, first_tap * L : (first_tap + n_taps) * L],
                in_=up_ps[:].rearrange("p k l -> p (k l)"),
                func=IDENTITY,
                bias=bias_cols[:, h : h + 1],
            )

        grouped_tiles = [regroup_wt(PIECES[0])]
        up_ps_tiles = []
        for i in range(len(PIECES)):
            if i + 1 < len(PIECES):
                grouped_tiles.append(regroup_wt(PIECES[i + 1]))
            up_ps_tiles.append(quantise_and_multiply(PIECES[i], grouped_tiles[i]))
            if i >= 1:
                add_bt(PIECES[i - 1], up_ps_tiles[i - 1])
            if i + 1 == CHUNKS_BEFORE_W1:
                transpose_w1()
            if i == CHUNKS_BEFORE_W1:
                regroup_w1()
        quantise_w1()

        up_grouped = const.tile([P, HALVES, HALF_T, PACK], BF16, align_bytes=64)
        up_codes = const.tile([P, T], U32, align_bytes=64)
        up_scales = const.tile([P, T], U8, align_bytes=64)
        src = up_planes[:].rearrange("p h (f c i) -> p f c h i", f=HALVES, i=4)
        dst = up_grouped[:].rearrange("p f (c i) h -> p f c h i", i=4)
        split = UP_VECTOR_STEPS // 4
        nc.vector.tensor_copy(out=dst[:, 0], in_=src[:, 0])
        add_bt(PIECES[-1], up_ps_tiles[-1])
        nc.vector.tensor_copy(out=dst[:, 1, 0:split], in_=src[:, 1, 0:split])
        nc.scalar.copy(out=dst[:, 1, split : HALF_T // 4], in_=src[:, 1, split : HALF_T // 4])
        for half in range(HALVES):
            steps = slice(half * HALF_T, (half + 1) * HALF_T)
            nc.vector.quantize_mx(
                out=up_codes[:, steps].bitcast(FP8X4),
                scales=up_scales[:, steps],
                in_=up_grouped[:, half].rearrange("p s h -> p (s h)"),
            )

        out_rows = out.rearrange("j b n s -> (j b n) s")
        for a in range(Y_TILES):
            rows = slice(a * P, (a + 1) * P)
            y_ps = psum_y.tile([P, T], F32)
            for half in range(HALVES):
                steps = slice(half * HALF_T, (half + 1) * HALF_T)
                nc.tensor.matmul_mx(
                    out=y_ps[:, steps],
                    lhsT=w1_codes[:, rows].bitcast(FP8X4),
                    lhsT_scale=w1_scales[:, rows],
                    rhs=up_codes[:, steps].bitcast(FP8X4),
                    rhs_scale=up_scales[:, steps],
                    start=True,
                    stop=True,
                )
            y_sb = results.tile([P, T], F32)
            y_in_time = y_sb[:].rearrange("p (l k) -> p l k", k=TAPS)
            y_by_tap = y_ps[:].rearrange("p (k l) -> p l k", k=TAPS)
            b1_col = bias_cols[:, O_TILES + a : O_TILES + a + 1]
            if a % 2 == 0:
                nc.vector.tensor_scalar_add(out=y_in_time, in0=y_by_tap, scalar1=b1_col)
            else:
                nc.scalar.activation(out=y_in_time, in_=y_by_tap, func=IDENTITY, bias=b1_col)
            for r in range(REPEAT):
                nc.sync.dma_start(out=out_rows[rows, r * T : (r + 1) * T], in_=y_sb[:])
